import numpy as np
import ml_dtypes


def mxq(x, axis, fmt="e4m3"):
    dtype, down = {"e4m3": (ml_dtypes.float8_e4m3fn, 7), "e5m2": (ml_dtypes.float8_e5m2, 14)}[fmt]
    v = np.moveaxis(np.asarray(x, np.float32).astype(ml_dtypes.bfloat16).astype(np.float64), axis, -1)
    blocks = v.reshape(v.shape[:-1] + (-1, 32))
    amax = np.abs(blocks).max(-1, keepdims=True)
    byte = np.maximum(np.where(amax > 0, np.frexp(amax)[1] - 1 + 127, 0) - down, 1)
    scale = np.exp2(byte - 127.0)
    codes = (blocks / scale).astype(np.float32).astype(dtype).astype(np.float64)
    return np.moveaxis((codes * scale).reshape(v.shape), -1, axis)


WIDE = False


def mx_kscale(k):
    if not WIDE:
        return np.ones(k)
    levels = np.array([10, -10, 5, -5, 0])
    a = np.random.permutation(np.resize(levels, k // 512 * 4)).reshape(k // 512, 4)
    idx = np.arange(k)
    return np.exp2(a[idx // 512, idx % 128 // 32])


BF16 = ml_dtypes.bfloat16


def bf(x):
    return np.asarray(x, np.float32).astype(BF16)


def f64(x):
    return np.asarray(x).astype(np.float64)


B, S, C, H = 4, 1024, 512, 4096
WS = 1.25


def setup_inputs():
    s = mx_kscale(C)
    return {"x": bf(np.random.standard_normal((B, S, C)) * s),
            "w_qk": bf(np.random.standard_normal((2 * C, C)) * WS / np.sqrt(C) / s[None, :])}


def reference(x, w_qk):
    qk = mxq(f64(w_qk), 1, "e4m3") @ mxq(f64(x), 2, "e4m3").transpose(0, 2, 1)
    q, k = qk[:, :C, :], qk[:, C:, :]
    return (mxq(q, 2, "e4m3") @ mxq(k, 2, "e4m3").transpose(0, 2, 1)) / np.sqrt(S)

@@ -1,0 +1,150 @@
+import math
+from contextlib import ExitStack
+
+import concourse.mybir as mybir
+from concourse.masks import make_identity
+
+BF16 = mybir.dt.bfloat16
+F32 = mybir.dt.float32
+U32 = mybir.dt.uint32
+U8 = mybir.dt.uint8
+FP8X4 = mybir.dt.float8_e4m3fn_x4
+
+P = 128
+PACK = 4
+K_PASS = P * PACK
+
+B, S, C = 4, 1024, 512
+S_PASSES = S // K_PASS
+UNITS = B * S_PASSES
+WORDS = C // 2
+M_TILES = C // P
+
+FLOPS = 2 * B * (2 * C) * S * C + 2 * B * C * C * S
+
+
+def tile_transformer_block_pa_t_kernel(tc, x, w_qk, out):
+    nc = tc.nc
+    with ExitStack() as ctx:
+        ctx.enter_context(tc.manual_schedule())
+        const = ctx.enter_context(tc.tile_pool(name="const", bufs=1))
+        raw_pool = ctx.enter_context(tc.tile_pool(name="raw", bufs=UNITS + 2))
+        in_mx = ctx.enter_context(tc.tile_pool(name="in_mx", bufs=UNITS + 2))
+        stage = ctx.enter_context(tc.tile_pool(name="stage", bufs=3))
+        qk_mx = ctx.enter_context(tc.tile_pool(name="qk_mx", bufs=4 * S_PASSES))
+        results = ctx.enter_context(tc.tile_pool(name="results", bufs=4))
+        psum_t = ctx.enter_context(tc.psum_pool(name="psum_t", bufs=2))
+        psum_1 = ctx.enter_context(tc.psum_pool(name="psum_1", bufs=4))
+        psum_2 = ctx.enter_context(tc.psum_pool(name="psum_2", bufs=2))
+
+        def load_x(n):
+            raw = raw_pool.tile([P, PACK * C], BF16)
+            rows = x.flatten_outer_dims()[n * K_PASS : (n + 1) * K_PASS, :]
+            nc.sync.dma_start(out=raw[:], in_=rows.rearrange("(p j) c -> p (j c)", j=PACK))
+            return raw
+
+        def load_w(h):
+            raw = raw_pool.tile([P, PACK * C], BF16)
+            rows = w_qk[h * K_PASS : (h + 1) * K_PASS, :]
+            nc.sync.dma_start(
+                out=raw[:].rearrange("p (t c) -> p t c", t=PACK),
+                in_=rows.rearrange("(t p) c -> p t c", p=P),
+            )
+            return raw
+
+        x_raw = [load_x(0)]
+        w_raw = [load_w(0), load_w(1)]
+        for n in range(1, UNITS):
+            x_raw.append(load_x(n))
+
+        identity = const.tile([P, P], F32)
+        make_identity(nc, identity[:])
+
+        def transpose_unit(raw, copy_out):
+            raw_words = raw[:].bitcast(F32)
+            grouped = stage.tile([P, K_PASS * PACK], BF16, align_bytes=64)
+            grouped_words = grouped[:].bitcast(F32).rearrange("p (r u) -> p r u", u=2)
+            for pair in range(PACK // 2):
+                bank = psum_t.tile([P, 2, 2 * P], F32)
+                for t in range(2):
+                    for u in range(2):
+                        first = (2 * pair + t) * WORDS + u * P
+                        nc.tensor.transpose(
+                            bank[:, u, t * P : (t + 1) * P], raw_words[:, first : first + P], identity[:]
+                        )
+                copy_out(
+                    out=grouped_words[:, 2 * pair * P : 2 * (pair + 1) * P, :],
+                    in_=bank[:].rearrange("p u r -> p r u"),
+                )
+            return grouped[:]
+
+        def quantise(pool, grouped):
+            codes = pool.tile([P, K_PASS], U32, align_bytes=64)
+            scales = pool.tile([P, K_PASS], U8, align_bytes=64)
+            nc.vector.quantize_mx(out=codes[:].bitcast(FP8X4), scales=scales[:], in_=grouped)
+            return codes, scales
+
+        def first_matmul(x_unit, w_half):
+            x_codes, x_scales = x_unit
+            w_codes, w_scales = w_half
+            qk_grouped = stage.tile([P, K_PASS, PACK], BF16, align_bytes=64)
+            for t in range(PACK):
+                channels = slice(t * P, (t + 1) * P)
+                bank_1 = psum_1.tile([P, PACK, P], F32)
+                for j in range(PACK):
+                    tokens = slice(j * P, (j + 1) * P)
+                    nc.tensor.matmul_mx(
+                        out=bank_1[:, j, :],
+                        lhsT=x_codes[:, tokens].bitcast(FP8X4),
+                        lhsT_scale=x_scales[:, tokens],
+                        rhs=w_codes[:, channels].bitcast(FP8X4),
+                        rhs_scale=w_scales[:, channels],
+                        start=True,
+                        stop=True,
+                    )
+                nc.scalar.copy(out=qk_grouped[:, channels, :], in_=bank_1[:].rearrange("p j o -> p o j"))
+            return qk_grouped[:].rearrange("p o j -> p (o j)")
+
+        def second_matmul(b, m_tiles):
+            for m in m_tiles:
+                rows = slice(m * P, (m + 1) * P)
+                acc = psum_2.tile([P, C], F32)
+                for g in range(S_PASSES):
+                    q_codes, q_scales = q_units[b * S_PASSES + g]
+                    k_codes, k_scales = k_units[b * S_PASSES + g]
+                    nc.tensor.matmul_mx(
+                        out=acc[:],
+                        lhsT=q_codes[:, rows].bitcast(FP8X4),
+                        lhsT_scale=q_scales[:, rows],
+                        rhs=k_codes[:].bitcast(FP8X4),
+                        rhs_scale=k_scales[:],
+                        start=(g == 0),
+                        stop=(g == S_PASSES - 1),
+                    )
+                score = results.tile([P, C], F32)
+                nc.vector.tensor_scalar_mul(out=score[:], in0=acc[:], scalar1=1.0 / math.sqrt(S))
+                nc.sync.dma_start(out=out[b, rows, :], in_=score[:])
+
+        x_units = [quantise(in_mx, transpose_unit(x_raw[0], nc.vector.tensor_copy))]
+        w_halves = [quantise(in_mx, transpose_unit(w_raw[h], nc.scalar.copy)) for h in range(2)]
+        q_units = []
+        k_units = []
+        k_grouped = None
+        for n in range(UNITS):
+            b, g = divmod(n, S_PASSES)
+
+            q_grouped = first_matmul(x_units[n], w_halves[0])
+            if n + 1 < UNITS:
+                x_grouped = transpose_unit(x_raw[n + 1], nc.vector.tensor_copy)
+            if n > 0:
+                k_units.append(quantise(qk_mx, k_grouped))
+            if n + 1 < UNITS:
+                x_units.append(quantise(in_mx, x_grouped))
+
+            k_grouped = first_matmul(x_units[n], w_halves[1])
+            q_units.append(quantise(qk_mx, q_grouped))
+            if b > 0:
+                second_matmul(b - 1, range(g * M_TILES // 2, (g + 1) * M_TILES // 2))
+
+        k_units.append(quantise(qk_mx, k_grouped))
+        second_matmul(B - 1, range(M_TILES))

@@ -18,7 +18,13 @@ B, S, C = 4, 1024, 512
 S_PASSES = S // K_PASS
 UNITS = B * S_PASSES
 WORDS = C // 2
+PIECE = 2 * P
+PIECES = K_PASS // PIECE
 M_TILES = C // P
+PSUM_BANKS = 8
+Q, K = 0, 1
+
+VECTOR_EVERY = 5
 
 FLOPS = 2 * B * (2 * C) * S * C + 2 * B * C * C * S
 
@@ -28,69 +34,75 @@ def tile_transformer_block_pa_t_kernel(tc, x, w_qk, out):
     with ExitStack() as ctx:
         ctx.enter_context(tc.manual_schedule())
         const = ctx.enter_context(tc.tile_pool(name="const", bufs=1))
-        raw_pool = ctx.enter_context(tc.tile_pool(name="raw", bufs=UNITS + 2))
+        raw_pool = ctx.enter_context(tc.tile_pool(name="raw", bufs=(UNITS + 2) * PIECES))
         in_mx = ctx.enter_context(tc.tile_pool(name="in_mx", bufs=UNITS + 2))
-        stage = ctx.enter_context(tc.tile_pool(name="stage", bufs=3))
+        stage = ctx.enter_context(tc.tile_pool(name="stage", bufs=4))
         qk_mx = ctx.enter_context(tc.tile_pool(name="qk_mx", bufs=4 * S_PASSES))
-        results = ctx.enter_context(tc.tile_pool(name="results", bufs=4))
-        psum_t = ctx.enter_context(tc.psum_pool(name="psum_t", bufs=2))
-        psum_1 = ctx.enter_context(tc.psum_pool(name="psum_1", bufs=4))
-        psum_2 = ctx.enter_context(tc.psum_pool(name="psum_2", bufs=2))
+        results = ctx.enter_context(tc.tile_pool(name="results", bufs=2 * M_TILES))
+        psum = ctx.enter_context(tc.psum_pool(name="psum", bufs=PSUM_BANKS))
+
+        def load(rows):
+            raw = raw_pool.tile([P, 2 * C], BF16)
+            nc.sync.dma_start(out=raw[:].rearrange("p (t c) -> p t c", t=2), in_=rows)
+            return raw
 
         def load_x(n):
-            raw = raw_pool.tile([P, PACK * C], BF16)
-            rows = x.flatten_outer_dims()[n * K_PASS : (n + 1) * K_PASS, :]
-            nc.sync.dma_start(out=raw[:], in_=rows.rearrange("(p j) c -> p (j c)", j=PACK))
-            return raw
+            unit = x.flatten_outer_dims()[n * K_PASS : (n + 1) * K_PASS, :]
+            by_partition = unit.rearrange("(p j) c -> p j c", j=PACK)
+            return [load(by_partition[:, 2 * i : 2 * i + 2, :]) for i in range(PIECES)]
 
-        def load_w(h):
-            raw = raw_pool.tile([P, PACK * C], BF16)
-            rows = w_qk[h * K_PASS : (h + 1) * K_PASS, :]
-            nc.sync.dma_start(
-                out=raw[:].rearrange("p (t c) -> p t c", t=PACK),
-                in_=rows.rearrange("(t p) c -> p t c", p=P),
-            )
-            return raw
+        def load_w(half):
+            by_partition = w_qk[half * C : (half + 1) * C, :].rearrange("(t p) c -> p t c", p=P)
+            return [load(by_partition[:, 2 * i : 2 * i + 2, :]) for i in range(PIECES)]
 
-        x_raw = [load_x(0)]
-        w_raw = [load_w(0), load_w(1)]
+        x_raw = {0: load_x(0)}
+        w_raw = {K: load_w(K), Q: load_w(Q)}
         for n in range(1, UNITS):
-            x_raw.append(load_x(n))
+            x_raw[n] = load_x(n)
 
         identity = const.tile([P, P], F32)
         make_identity(nc, identity[:])
 
-        def transpose_unit(raw, copy_out):
-            raw_words = raw[:].bitcast(F32)
-            grouped = stage.tile([P, K_PASS * PACK], BF16, align_bytes=64)
-            grouped_words = grouped[:].bitcast(F32).rearrange("p (r u) -> p r u", u=2)
-            for pair in range(PACK // 2):
-                bank = psum_t.tile([P, 2, 2 * P], F32)
-                for t in range(2):
-                    for u in range(2):
-                        first = (2 * pair + t) * WORDS + u * P
-                        nc.tensor.transpose(
-                            bank[:, u, t * P : (t + 1) * P], raw_words[:, first : first + P], identity[:]
-                        )
-                copy_out(
-                    out=grouped_words[:, 2 * pair * P : 2 * (pair + 1) * P, :],
-                    in_=bank[:].rearrange("p u r -> p r u"),
-                )
-            return grouped[:]
-
-        def quantise(pool, grouped):
+        def new_mx(pool):
             codes = pool.tile([P, K_PASS], U32, align_bytes=64)
             scales = pool.tile([P, K_PASS], U8, align_bytes=64)
-            nc.vector.quantize_mx(out=codes[:].bitcast(FP8X4), scales=scales[:], in_=grouped)
             return codes, scales
 
-        def first_matmul(x_unit, w_half):
-            x_codes, x_scales = x_unit
-            w_codes, w_scales = w_half
-            qk_grouped = stage.tile([P, K_PASS, PACK], BF16, align_bytes=64)
-            for t in range(PACK):
+        def quantise(mx, columns, grouped):
+            codes, scales = mx
+            nc.vector.quantize_mx(
+                out=codes[:, columns].bitcast(FP8X4),
+                scales=scales[:, columns],
+                in_=grouped.rearrange("p r j -> p (r j)"),
+            )
+
+        def transpose_piece(raw, copy_out):
+            raw_words = raw[:].bitcast(F32)
+            bank_t = psum.tile([P, 2, PIECE], F32, tag="bank")
+            for t in range(2):
+                for u in range(2):
+                    first = t * WORDS + u * P
+                    nc.tensor.transpose(
+                        bank_t[:, u, t * P : (t + 1) * P], raw_words[:, first : first + P], identity[:]
+                    )
+            grouped = stage.tile([P, PIECE, PACK], BF16, align_bytes=64)
+            copy_out(
+                out=grouped[:].rearrange("p r j -> p (r j)").bitcast(F32).rearrange("p (r u) -> p r u", u=2),
+                in_=bank_t[:].rearrange("p u r -> p r u"),
+            )
+            return grouped
+
+        def quantise_pieces(mx, pieces):
+            for i in range(PIECES):
+                quantise(mx, slice(i * PIECE, (i + 1) * PIECE), pieces[i][:])
+
+        def first_matmul(n, half):
+            x_codes, x_scales = x_units[n]
+            w_codes, w_scales = w_halves[half]
+            qk_grouped = stage.tile([P, C, PACK], BF16, align_bytes=64)
+            for t in range(M_TILES):
                 channels = slice(t * P, (t + 1) * P)
-                bank_1 = psum_1.tile([P, PACK, P], F32)
+                bank_1 = psum.tile([P, PACK, P], F32, tag="bank")
                 for j in range(PACK):
                     tokens = slice(j * P, (j + 1) * P)
                     nc.tensor.matmul_mx(
@@ -102,49 +114,71 @@ def tile_transformer_block_pa_t_kernel(tc, x, w_qk, out):
                         start=True,
                         stop=True,
                     )
-                nc.scalar.copy(out=qk_grouped[:, channels, :], in_=bank_1[:].rearrange("p j o -> p o j"))
-            return qk_grouped[:].rearrange("p o j -> p (o j)")
+                banks_before = (2 * n + (1 - half)) * M_TILES + t
+                to_vector = banks_before % VECTOR_EVERY == VECTOR_EVERY - 1
+                copy_out = nc.vector.tensor_copy if to_vector else nc.scalar.copy
+                copy_out(out=qk_grouped[:, channels, :], in_=bank_1[:].rearrange("p j o -> p o j"))
+            return qk_grouped
 
-        def second_matmul(b, m_tiles):
-            for m in m_tiles:
-                rows = slice(m * P, (m + 1) * P)
-                acc = psum_2.tile([P, C], F32)
-                for g in range(S_PASSES):
-                    q_codes, q_scales = q_units[b * S_PASSES + g]
-                    k_codes, k_scales = k_units[b * S_PASSES + g]
-                    nc.tensor.matmul_mx(
-                        out=acc[:],
-                        lhsT=q_codes[:, rows].bitcast(FP8X4),
-                        lhsT_scale=q_scales[:, rows],
-                        rhs=k_codes[:].bitcast(FP8X4),
-                        rhs_scale=k_scales[:],
-                        start=(g == 0),
-                        stop=(g == S_PASSES - 1),
-                    )
-                score = results.tile([P, C], F32)
+        def second_matmul(b, m):
+            rows = slice(m * P, (m + 1) * P)
+            acc = psum.tile([P, C], F32, tag="bank")
+            for g in range(S_PASSES):
+                q_codes, q_scales = q_units[b * S_PASSES + g]
+                k_codes, k_scales = k_units[b * S_PASSES + g]
+                nc.tensor.matmul_mx(
+                    out=acc[:],
+                    lhsT=q_codes[:, rows].bitcast(FP8X4),
+                    lhsT_scale=q_scales[:, rows],
+                    rhs=k_codes[:].bitcast(FP8X4),
+                    rhs_scale=k_scales[:],
+                    start=(g == 0),
+                    stop=(g == S_PASSES - 1),
+                )
+            score = results.tile([P, C], F32)
+            if m % 2 == 0:
                 nc.vector.tensor_scalar_mul(out=score[:], in0=acc[:], scalar1=1.0 / math.sqrt(S))
-                nc.sync.dma_start(out=out[b, rows, :], in_=score[:])
+            else:
+                nc.scalar.mul(out=score[:], in_=acc[:], mul=1.0 / math.sqrt(S))
+            nc.sync.dma_start(out=out[b, rows, :], in_=score[:])
 
-        x_units = [quantise(in_mx, transpose_unit(x_raw[0], nc.vector.tensor_copy))]
-        w_halves = [quantise(in_mx, transpose_unit(w_raw[h], nc.scalar.copy)) for h in range(2)]
-        q_units = []
-        k_units = []
-        k_grouped = None
+        x_units = {}
+        w_halves = {}
+        q_units = {}
+        k_units = {}
+        whole = slice(0, C)
+
+        x_pieces = [transpose_piece(raw, nc.vector.tensor_copy) for raw in x_raw[0]]
+        x_units[0] = new_mx(in_mx)
+        quantise_pieces(x_units[0], x_pieces)
+        for half in (K, Q):
+            w_pieces = [transpose_piece(raw, nc.scalar.copy) for raw in w_raw[half]]
+            w_halves[half] = new_mx(in_mx)
+            quantise_pieces(w_halves[half], w_pieces)
+
+        q_grouped = None
         for n in range(UNITS):
             b, g = divmod(n, S_PASSES)
 
-            q_grouped = first_matmul(x_units[n], w_halves[0])
-            if n + 1 < UNITS:
-                x_grouped = transpose_unit(x_raw[n + 1], nc.vector.tensor_copy)
+            k_grouped = first_matmul(n, K)
             if n > 0:
-                k_units.append(quantise(qk_mx, k_grouped))
+                q_units[n - 1] = new_mx(qk_mx)
+                quantise(q_units[n - 1], whole, q_grouped[:])
             if n + 1 < UNITS:
-                x_units.append(quantise(in_mx, x_grouped))
+                x_pieces = [transpose_piece(raw, nc.vector.tensor_copy) for raw in x_raw[n + 1]]
+                x_units[n + 1] = new_mx(in_mx)
+                quantise_pieces(x_units[n + 1], x_pieces)
 
-            k_grouped = first_matmul(x_units[n], w_halves[1])
-            q_units.append(quantise(qk_mx, q_grouped))
+            q_grouped = first_matmul(n, Q)
+            k_units[n] = new_mx(qk_mx)
+            quantise(k_units[n], whole, k_grouped[:])
             if b > 0:
-                second_matmul(b - 1, range(g * M_TILES // 2, (g + 1) * M_TILES // 2))
+                for m in range(g * M_TILES // 2, (g + 1) * M_TILES // 2):
+                    second_matmul(b - 1, m)
 
-        k_units.append(quantise(qk_mx, k_grouped))
-        second_matmul(B - 1, range(M_TILES))
+        q_units[UNITS - 1] = new_mx(qk_mx)
+        for m in range(M_TILES):
+            channels = slice(m * P, (m + 1) * P)
+            quantise(q_units[UNITS - 1], channels, q_grouped[:, channels, :])
+        for m in range(M_TILES):
+            second_matmul(B - 1, m)

@@ -24,7 +24,7 @@ M_TILES = C // P
 PSUM_BANKS = 8
 Q, K = 0, 1
 
-VECTOR_EVERY = 5
+VECTOR_EVERY = 4
 
 FLOPS = 2 * B * (2 * C) * S * C + 2 * B * C * C * S
 
@@ -37,6 +37,7 @@ def tile_transformer_block_pa_t_kernel(tc, x, w_qk, out):
         raw_pool = ctx.enter_context(tc.tile_pool(name="raw", bufs=(UNITS + 2) * PIECES))
         in_mx = ctx.enter_context(tc.tile_pool(name="in_mx", bufs=UNITS + 2))
         stage = ctx.enter_context(tc.tile_pool(name="stage", bufs=4))
+        pieces_pool = ctx.enter_context(tc.tile_pool(name="pieces", bufs=4 * PIECES))
         qk_mx = ctx.enter_context(tc.tile_pool(name="qk_mx", bufs=4 * S_PASSES))
         results = ctx.enter_context(tc.tile_pool(name="results", bufs=2 * M_TILES))
         psum = ctx.enter_context(tc.psum_pool(name="psum", bufs=PSUM_BANKS))
@@ -85,7 +86,7 @@ def tile_transformer_block_pa_t_kernel(tc, x, w_qk, out):
                     nc.tensor.transpose(
                         bank_t[:, u, t * P : (t + 1) * P], raw_words[:, first : first + P], identity[:]
                     )
-            grouped = stage.tile([P, PIECE, PACK], BF16, align_bytes=64)
+            grouped = pieces_pool.tile([P, PIECE, PACK], BF16, align_bytes=64)
             copy_out(
                 out=grouped[:].rearrange("p r j -> p (r j)").bitcast(F32).rearrange("p (r u) -> p r u", u=2),
                 in_=bank_t[:].rearrange("p u r -> p r u"),
@@ -114,8 +115,7 @@ def tile_transformer_block_pa_t_kernel(tc, x, w_qk, out):
                         start=True,
                         stop=True,
                     )
-                banks_before = (2 * n + (1 - half)) * M_TILES + t
-                to_vector = banks_before % VECTOR_EVERY == VECTOR_EVERY - 1
+                to_vector = t % VECTOR_EVERY == VECTOR_EVERY - 1
                 copy_out = nc.vector.tensor_copy if to_vector else nc.scalar.copy
                 copy_out(out=qk_grouped[:, channels, :], in_=bank_1[:].rearrange("p j o -> p o j"))
             return qk_grouped
@@ -148,7 +148,13 @@ def tile_transformer_block_pa_t_kernel(tc, x, w_qk, out):
         k_units = {}
         whole = slice(0, C)
 
-        x_pieces = [transpose_piece(raw, nc.vector.tensor_copy) for raw in x_raw[0]]
+        def transpose_x(n):
+            return [
+                transpose_piece(x_raw[n][0], nc.vector.tensor_copy),
+                transpose_piece(x_raw[n][1], nc.scalar.copy),
+            ]
+
+        x_pieces = transpose_x(0)
         x_units[0] = new_mx(in_mx)
         quantise_pieces(x_units[0], x_pieces)
         for half in (K, Q):
@@ -164,10 +170,12 @@ def tile_transformer_block_pa_t_kernel(tc, x, w_qk, out):
             if n > 0:
                 q_units[n - 1] = new_mx(qk_mx)
                 quantise(q_units[n - 1], whole, q_grouped[:])
-            if n + 1 < UNITS:
-                x_pieces = [transpose_piece(raw, nc.vector.tensor_copy) for raw in x_raw[n + 1]]
-                x_units[n + 1] = new_mx(in_mx)
-                quantise_pieces(x_units[n + 1], x_pieces)
+            if g == 0:
+                ahead = [u for u in (n + 1, n + 2) if u < UNITS]
+                pieces_ahead = [transpose_x(u) for u in ahead]
+                for u, x_pieces in zip(ahead, pieces_ahead):
+                    x_units[u] = new_mx(in_mx)
+                    quantise_pieces(x_units[u], x_pieces)
 
             q_grouped = first_matmul(n, Q)
             k_units[n] = new_mx(qk_mx)

@@ -26,6 +26,8 @@ Q, K = 0, 1
 
 VECTOR_EVERY = 4
 
+WARM_PASSES = 16
+
 FLOPS = 2 * B * (2 * C) * S * C + 2 * B * C * C * S
 
 
@@ -60,6 +62,12 @@ def tile_transformer_block_pa_t_kernel(tc, x, w_qk, out):
         w_raw = {K: load_w(K), Q: load_w(Q)}
         for n in range(1, UNITS):
             x_raw[n] = load_x(n)
+
+        zeros = const.tile([P, P], BF16)
+        nc.gpsimd.memset(zeros[:], 0.0)
+        unused = psum.tile([P, P], F32, tag="bank")
+        for _ in range(WARM_PASSES):
+            nc.tensor.matmul(out=unused[:], lhsT=zeros[:], rhs=zeros[:], start=True, stop=True)
 
         identity = const.tile([P, P], F32)
         make_identity(nc, identity[:])

@@ -55,7 +55,7 @@ def tile_transformer_block_pa_t_kernel(tc, x, w_qk, out):
             return [load(by_partition[:, 2 * i : 2 * i + 2, :]) for i in range(PIECES)]
 
         def load_w(half):
-            by_partition = w_qk[half * C : (half + 1) * C, :].rearrange("(t p) c -> p t c", p=P)
+            by_partition = w_qk[half * C : (half + 1) * C, :].rearrange("(p t) c -> p t c", t=M_TILES)
             return [load(by_partition[:, 2 * i : 2 * i + 2, :]) for i in range(PIECES)]
 
         x_raw = {0: load_x(0)}
@@ -144,11 +144,13 @@ def tile_transformer_block_pa_t_kernel(tc, x, w_qk, out):
                     stop=(g == S_PASSES - 1),
                 )
             score = results.tile([P, C], F32)
+            in_order = score[:].rearrange("p (o t) -> p o t", t=M_TILES)
+            as_computed = acc[:].rearrange("p (t o) -> p o t", t=M_TILES)
             if m % 2 == 0:
-                nc.vector.tensor_scalar_mul(out=score[:], in0=acc[:], scalar1=1.0 / math.sqrt(S))
+                nc.vector.tensor_scalar_mul(out=in_order, in0=as_computed, scalar1=1.0 / math.sqrt(S))
             else:
-                nc.scalar.mul(out=score[:], in_=acc[:], mul=1.0 / math.sqrt(S))
-            nc.sync.dma_start(out=out[b, rows, :], in_=score[:])
+                nc.scalar.mul(out=in_order, in_=as_computed, mul=1.0 / math.sqrt(S))
+            nc.sync.dma_start(out=out[b].rearrange("(p t) n -> t p n", t=M_TILES)[m], in_=score[:])
 
         x_units = {}
         w_halves = {}
@@ -166,7 +168,11 @@ def tile_transformer_block_pa_t_kernel(tc, x, w_qk, out):
         x_units[0] = new_mx(in_mx)
         quantise_pieces(x_units[0], x_pieces)
         for half in (K, Q):
-            w_pieces = [transpose_piece(raw, nc.scalar.copy) for raw in w_raw[half]]
+            last_copy = nc.vector.tensor_copy if half == Q else nc.scalar.copy
+            w_pieces = [
+                transpose_piece(w_raw[half][0], nc.scalar.copy),
+                transpose_piece(w_raw[half][1], last_copy),
+            ]
             w_halves[half] = new_mx(in_mx)
             quantise_pieces(w_halves[half], w_pieces)
 

@@ -36,7 +36,8 @@ def tile_transformer_block_pa_t_kernel(tc, x, w_qk, out):
     with ExitStack() as ctx:
         ctx.enter_context(tc.manual_schedule())
         const = ctx.enter_context(tc.tile_pool(name="const", bufs=1))
-        raw_pool = ctx.enter_context(tc.tile_pool(name="raw", bufs=(UNITS + 2) * PIECES))
+        raw_pool = ctx.enter_context(tc.tile_pool(name="raw", bufs=3 * PIECES))
+        raw_units = ctx.enter_context(tc.tile_pool(name="raw_units", bufs=UNITS - 1))
         in_mx = ctx.enter_context(tc.tile_pool(name="in_mx", bufs=UNITS + 2))
         stage = ctx.enter_context(tc.tile_pool(name="stage", bufs=4))
         pieces_pool = ctx.enter_context(tc.tile_pool(name="pieces", bufs=4 * PIECES))
@@ -47,12 +48,16 @@ def tile_transformer_block_pa_t_kernel(tc, x, w_qk, out):
         def load(rows):
             raw = raw_pool.tile([P, 2 * C], BF16)
             nc.sync.dma_start(out=raw[:].rearrange("p (t c) -> p t c", t=2), in_=rows)
-            return raw
+            return raw[:]
 
         def load_x(n):
             unit = x.flatten_outer_dims()[n * K_PASS : (n + 1) * K_PASS, :]
             by_partition = unit.rearrange("(p j) c -> p j c", j=PACK)
-            return [load(by_partition[:, 2 * i : 2 * i + 2, :]) for i in range(PIECES)]
+            if n == 0:
+                return [load(by_partition[:, 2 * i : 2 * i + 2, :]) for i in range(PIECES)]
+            raw_unit = raw_units.tile([P, PACK * C], BF16)
+            nc.sync.dma_start(out=raw_unit[:].rearrange("p (j c) -> p j c", j=PACK), in_=by_partition)
+            return [raw_unit[:, 2 * i * C : 2 * (i + 1) * C] for i in range(PIECES)]
 
         def load_w(half):
             by_partition = w_qk[half * C : (half + 1) * C, :].rearrange("(p t) c -> p t c", t=M_TILES)
@@ -86,7 +91,7 @@ def tile_transformer_block_pa_t_kernel(tc, x, w_qk, out):
             )
 
         def transpose_piece(raw, copy_out):
-            raw_words = raw[:].bitcast(F32)
+            raw_words = raw.bitcast(F32)
             bank_t = psum.tile([P, 2, PIECE], F32, tag="bank")
             for t in range(2):
                 for u in range(2):

import math
from contextlib import ExitStack

import concourse.mybir as mybir
from concourse.masks import make_identity

BF16 = mybir.dt.bfloat16
F32 = mybir.dt.float32
U32 = mybir.dt.uint32
U8 = mybir.dt.uint8
FP8X4 = mybir.dt.float8_e4m3fn_x4

P = 128
PACK = 4
K_PASS = P * PACK

B, S, C = 4, 1024, 512
S_PASSES = S // K_PASS
UNITS = B * S_PASSES
WORDS = C // 2
PIECE = 2 * P
PIECES = K_PASS // PIECE
M_TILES = C // P
PSUM_BANKS = 8
Q, K = 0, 1

VECTOR_EVERY = 4

WARM_PASSES = 16

FLOPS = 2 * B * (2 * C) * S * C + 2 * B * C * C * S


def tile_transformer_block_pa_t_kernel(tc, x, w_qk, out):
    nc = tc.nc
    with ExitStack() as ctx:
        ctx.enter_context(tc.manual_schedule())
        const = ctx.enter_context(tc.tile_pool(name="const", bufs=1))
        raw_pool = ctx.enter_context(tc.tile_pool(name="raw", bufs=3 * PIECES))
        raw_units = ctx.enter_context(tc.tile_pool(name="raw_units", bufs=UNITS - 1))
        in_mx = ctx.enter_context(tc.tile_pool(name="in_mx", bufs=UNITS + 2))
        stage = ctx.enter_context(tc.tile_pool(name="stage", bufs=4))
        pieces_pool = ctx.enter_context(tc.tile_pool(name="pieces", bufs=4 * PIECES))
        qk_mx = ctx.enter_context(tc.tile_pool(name="qk_mx", bufs=4 * S_PASSES))
        results = ctx.enter_context(tc.tile_pool(name="results", bufs=2 * M_TILES))
        psum = ctx.enter_context(tc.psum_pool(name="psum", bufs=PSUM_BANKS))

        def load(rows):
            raw = raw_pool.tile([P, 2 * C], BF16)
            nc.sync.dma_start(out=raw[:].rearrange("p (t c) -> p t c", t=2), in_=rows)
            return raw[:]

        def load_x(n):
            unit = x.flatten_outer_dims()[n * K_PASS : (n + 1) * K_PASS, :]
            by_partition = unit.rearrange("(p j) c -> p j c", j=PACK)
            if n == 0:
                return [load(by_partition[:, 2 * i : 2 * i + 2, :]) for i in range(PIECES)]
            raw_unit = raw_units.tile([P, PACK * C], BF16)
            nc.sync.dma_start(out=raw_unit[:].rearrange("p (j c) -> p j c", j=PACK), in_=by_partition)
            return [raw_unit[:, 2 * i * C : 2 * (i + 1) * C] for i in range(PIECES)]

        def load_w(half):
            by_partition = w_qk[half * C : (half + 1) * C, :].rearrange("(p t) c -> p t c", t=M_TILES)
            return [load(by_partition[:, 2 * i : 2 * i + 2, :]) for i in range(PIECES)]

        x_raw = {0: load_x(0)}
        w_raw = {K: load_w(K), Q: load_w(Q)}
        for n in range(1, UNITS):
            x_raw[n] = load_x(n)

        zeros = const.tile([P, P], BF16)
        nc.gpsimd.memset(zeros[:], 0.0)
        unused = psum.tile([P, P], F32, tag="bank")
        for _ in range(WARM_PASSES):
            nc.tensor.matmul(out=unused[:], lhsT=zeros[:], rhs=zeros[:], start=True, stop=True)

        identity = const.tile([P, P], F32)
        make_identity(nc, identity[:])

        def new_mx(pool):
            codes = pool.tile([P, K_PASS], U32, align_bytes=64)
            scales = pool.tile([P, K_PASS], U8, align_bytes=64)
            return codes, scales

        def quantise(mx, columns, grouped):
            codes, scales = mx
            nc.vector.quantize_mx(
                out=codes[:, columns].bitcast(FP8X4),
                scales=scales[:, columns],
                in_=grouped.rearrange("p r j -> p (r j)"),
            )

        def transpose_piece(raw, copy_out):
            raw_words = raw.bitcast(F32)
            bank_t = psum.tile([P, 2, PIECE], F32, tag="bank")
            for t in range(2):
                for u in range(2):
                    first = t * WORDS + u * P
                    nc.tensor.transpose(
                        bank_t[:, u, t * P : (t + 1) * P], raw_words[:, first : first + P], identity[:]
                    )
            grouped = pieces_pool.tile([P, PIECE, PACK], BF16, align_bytes=64)
            copy_out(
                out=grouped[:].rearrange("p r j -> p (r j)").bitcast(F32).rearrange("p (r u) -> p r u", u=2),
                in_=bank_t[:].rearrange("p u r -> p r u"),
            )
            return grouped

        def quantise_pieces(mx, pieces):
            for i in range(PIECES):
                quantise(mx, slice(i * PIECE, (i + 1) * PIECE), pieces[i][:])

        def first_matmul(n, half):
            x_codes, x_scales = x_units[n]
            w_codes, w_scales = w_halves[half]
            qk_grouped = stage.tile([P, C, PACK], BF16, align_bytes=64)
            for t in range(M_TILES):
                channels = slice(t * P, (t + 1) * P)
                bank_1 = psum.tile([P, PACK, P], F32, tag="bank")
                for j in range(PACK):
                    tokens = slice(j * P, (j + 1) * P)
                    nc.tensor.matmul_mx(
                        out=bank_1[:, j, :],
                        lhsT=x_codes[:, tokens].bitcast(FP8X4),
                        lhsT_scale=x_scales[:, tokens],
                        rhs=w_codes[:, channels].bitcast(FP8X4),
                        rhs_scale=w_scales[:, channels],
                        start=True,
                        stop=True,
                    )
                to_vector = t % VECTOR_EVERY == VECTOR_EVERY - 1
                copy_out = nc.vector.tensor_copy if to_vector else nc.scalar.copy
                copy_out(out=qk_grouped[:, channels, :], in_=bank_1[:].rearrange("p j o -> p o j"))
            return qk_grouped

        def second_matmul(b, m):
            rows = slice(m * P, (m + 1) * P)
            acc = psum.tile([P, C], F32, tag="bank")
            for g in range(S_PASSES):
                q_codes, q_scales = q_units[b * S_PASSES + g]
                k_codes, k_scales = k_units[b * S_PASSES + g]
                nc.tensor.matmul_mx(
                    out=acc[:],
                    lhsT=q_codes[:, rows].bitcast(FP8X4),
                    lhsT_scale=q_scales[:, rows],
                    rhs=k_codes[:].bitcast(FP8X4),
                    rhs_scale=k_scales[:],
                    start=(g == 0),
                    stop=(g == S_PASSES - 1),
                )
            score = results.tile([P, C], F32)
            in_order = score[:].rearrange("p (o t) -> p o t", t=M_TILES)
            as_computed = acc[:].rearrange("p (t o) -> p o t", t=M_TILES)
            if m % 2 == 0:
                nc.vector.tensor_scalar_mul(out=in_order, in0=as_computed, scalar1=1.0 / math.sqrt(S))
            else:
                nc.scalar.mul(out=in_order, in_=as_computed, mul=1.0 / math.sqrt(S))
            nc.sync.dma_start(out=out[b].rearrange("(p t) n -> t p n", t=M_TILES)[m], in_=score[:])

        x_units = {}
        w_halves = {}
        q_units = {}
        k_units = {}
        whole = slice(0, C)

        def transpose_x(n):
            return [
                transpose_piece(x_raw[n][0], nc.vector.tensor_copy),
                transpose_piece(x_raw[n][1], nc.scalar.copy),
            ]

        x_pieces = transpose_x(0)
        x_units[0] = new_mx(in_mx)
        quantise_pieces(x_units[0], x_pieces)
        for half in (K, Q):
            last_copy = nc.vector.tensor_copy if half == Q else nc.scalar.copy
            w_pieces = [
                transpose_piece(w_raw[half][0], nc.scalar.copy),
                transpose_piece(w_raw[half][1], last_copy),
            ]
            w_halves[half] = new_mx(in_mx)
            quantise_pieces(w_halves[half], w_pieces)

        q_grouped = None
        for n in range(UNITS):
            b, g = divmod(n, S_PASSES)

            k_grouped = first_matmul(n, K)
            if n > 0:
                q_units[n - 1] = new_mx(qk_mx)
                quantise(q_units[n - 1], whole, q_grouped[:])
            if g == 0:
                ahead = [u for u in (n + 1, n + 2) if u < UNITS]
                pieces_ahead = [transpose_x(u) for u in ahead]
                for u, x_pieces in zip(ahead, pieces_ahead):
                    x_units[u] = new_mx(in_mx)
                    quantise_pieces(x_units[u], x_pieces)

            q_grouped = first_matmul(n, Q)
            k_units[n] = new_mx(qk_mx)
            quantise(k_units[n], whole, k_grouped[:])
            if b > 0:
                for m in range(g * M_TILES // 2, (g + 1) * M_TILES // 2):
                    second_matmul(b - 1, m)

        q_units[UNITS - 1] = new_mx(qk_mx)
        for m in range(M_TILES):
            channels = slice(m * P, (m + 1) * P)
            quantise(q_units[UNITS - 1], channels, q_grouped[:, channels, :])
        for m in range(M_TILES):
            second_matmul(B - 1, m)
